import numpy as np
import ml_dtypes


BF16 = ml_dtypes.bfloat16


def bf(x):
    return np.asarray(x, np.float32).astype(BF16)


def f64(x):
    return np.asarray(x).astype(np.float64)


E2M1 = np.array([0.0, 0.5, 1.0, 1.5, 2.0, 3.0, 4.0, 6.0, -0.0, -0.5, -1.0, -1.5, -2.0, -3.0, -4.0, -6.0])


def pack_weight(w, fmt):
    k, n = w.shape
    w = f64(bf(w)).reshape(k // 32, 32, n)
    amax = np.abs(w).max(1)
    if fmt == "e4m3":
        byte = np.frexp(amax)[1] - 1 + 127 - 7
    else:
        mant, ex = np.frexp(amax / 6.0)
        byte = np.where(mant > 0.5, ex, ex - 1) + 127
    byte = np.clip(np.where(amax > 0, byte, 1), 1, 254)
    scaled = (w * np.exp2(127.0 - byte)[:, None, :]).reshape(k, n).astype(np.float32)
    by_word = np.ascontiguousarray(scaled.reshape(k // 512, 128, 4, n).transpose(0, 1, 3, 2))
    if fmt == "e4m3":
        words = by_word.astype(ml_dtypes.float8_e4m3fn).view(np.uint8)
    else:
        c = by_word.astype(ml_dtypes.float4_e2m1fn).view(np.uint8) & 0xF
        words = c[..., 0::2] | (c[..., 1::2] << 4)
    return np.ascontiguousarray(words), np.ascontiguousarray(byte.astype(np.uint8).reshape(k // 512, 16, n))


def unpack_weight(words, scales, fmt):
    g, p, n, _ = words.shape
    if fmt == "e4m3":
        vals = np.ascontiguousarray(words).view(ml_dtypes.float8_e4m3fn).astype(np.float64)
    else:
        nib = np.empty((g, p, n, 4), np.uint8)
        nib[..., 0::2] = words & 0xF
        nib[..., 1::2] = words >> 4
        vals = E2M1[nib]
    vals = vals * np.repeat(np.exp2(scales.astype(np.float64) - 127.0), 8, axis=1)[..., None]
    return vals.transpose(0, 1, 3, 2).reshape(g * 512, n)

def pack4(w):
    words, scales = pack_weight(w, "e2m1")
    return words.reshape(words.shape[0], 128, -1), scales


def unpack4(words, scales):
    return unpack_weight(words.reshape(words.shape[0], 128, -1, 2), scales, "e2m1")


def kspread(k):
    return np.exp2(np.repeat(np.random.randint(-6, 7, k // 32), 32).astype(np.float64))


B, L, E, H = 2, 64, 3584, 16
HD = E // H
EPS = 1e-12


def l2_normalize(t):
    n = np.sqrt(np.sum(t * t, axis=-1, keepdims=True))
    return t / np.maximum(n, EPS)


def setup_inputs():
    s = kspread(E)
    x = np.random.standard_normal((B, L, E)) * s
    x_words, x_scales = pack4(np.ascontiguousarray(x.reshape(B * L, E).T))
    w = np.random.standard_normal((3 * E, E)) / np.sqrt(E) / s[None, :]
    words, scales = pack4(np.ascontiguousarray(w.T))
    b = bf(np.random.standard_normal(3 * E) * 0.3)
    return {"x_words": x_words, "x_scales": x_scales, "W_words": words, "W_scales": scales, "b": b}


def reference(x_words, x_scales, W_words, W_scales, b):
    x = unpack4(x_words, x_scales).T.reshape(B, L, E)
    y = (x @ unpack4(W_words, W_scales)) + f64(b)
    y = y.reshape(B, L, H, 3, HD)
    q = np.transpose(y[..., 0, :], (0, 2, 1, 3))
    k = np.transpose(y[..., 1, :], (0, 2, 1, 3))
    v = np.transpose(y[..., 2, :], (0, 2, 1, 3))
    return l2_normalize(q), l2_normalize(k), v

@@ -1,0 +1,269 @@
+from contextlib import ExitStack
+
+import concourse.mybir as mybir
+from concourse.masks import make_identity
+
+F32 = mybir.dt.float32
+BF16 = mybir.dt.bfloat16
+U8 = mybir.dt.uint8
+I32 = mybir.dt.int32
+FP4X4 = mybir.dt.float4_e2m1fn_x4
+AF = mybir.ActivationFunctionType
+ALU = mybir.AluOpType
+
+P = 128
+PASSES = 7
+COLS = 10752
+SEG = 224
+THIRD = 3584
+SEGS = 48
+BANK = 512
+FLOPS = 2 * 128 * 3584 * 10752
+
+ONE_BY_ONE = tuple((g, g + 1) for g in range(PASSES))
+GROUPS = (
+    (3584, ONE_BY_ONE, True),
+    (3584, ONE_BY_ONE, True),
+    (1792, ONE_BY_ONE, True),
+    (1024, ONE_BY_ONE, False),
+    (512, ((0, 7),), False),
+    (256, ((0, 4), (4, 7)), False),
+)
+SCALES_BEFORE = (3, 5, 12)
+STORE_CUTS = (8, 16, 24, 32, 40, 44, 46, 48)
+LAST_ON_POOL = 32
+CODE_BUFS = 8
+LOOKAHEAD = 6
+
+
+def split_banks(width):
+    banks = []
+    at = 0
+    for n in (512, 256, 128):
+        while width - at >= n:
+            banks.append((at, n))
+            at += n
+    assert at == width
+    return banks
+
+
+def tile_selfattention_pa_kernel(tc, x_words, x_scales, W_words, W_scales, b, out_0, out_1, out_2):
+    nc = tc.nc
+    outs = (out_0, out_1, out_2)
+
+    with ExitStack() as ctx:
+        keep = ctx.enter_context(tc.tile_pool(name="keep", bufs=1))
+        stream = ctx.enter_context(tc.tile_pool(name="stream", bufs=CODE_BUFS))
+        psum = ctx.enter_context(tc.psum_pool(name="psum", bufs=1))
+        ctx.enter_context(tc.manual_schedule())
+
+        xw_raw = keep.tile([P, PASSES, 256], U8, name="xw_raw", tag="xw_raw", align_bytes=64)
+        xs_raw = keep.tile([P, PASSES, 128], U8, name="xs_raw", tag="xs_raw", align_bytes=64)
+        xw = keep.tile([P, PASSES, 256], U8, name="xw", tag="xw", align_bytes=64)
+        xs = keep.tile([P, PASSES, 128], U8, name="xs", tag="xs", align_bytes=64)
+        ident = keep.tile([P, P], BF16, name="ident", tag="ident")
+        brows = keep.tile([P, BANK], BF16, name="brows", tag="brows")
+        bias = keep.tile([P, COLS], BF16, name="bias", tag="bias")
+        ss = keep.tile([P, SEGS], F32, name="ss", tag="ss")
+        cl = keep.tile([P, SEGS], F32, name="cl", tag="cl")
+        rc = keep.tile([P, SEGS], F32, name="rc", tag="rc")
+        rn = keep.tile([P, SEGS], F32, name="rn", tag="rn")
+        junk = keep.tile([P, SEG], F32, name="junk", tag="junk")
+        warm = keep.tile([P, 1], F32, name="warm", tag="warm")
+        ys = []
+        planes = []
+        for t in range(3):
+            y_t = keep.tile([P, THIRD // SEG, SEG], F32, name="y%d" % t, tag="y%d" % t)
+            ys.append(y_t)
+            pl_t = keep.tile([P, PASSES, THIRD], U8, name="pl%d" % t, tag="pl%d" % t, align_bytes=64)
+            planes.append(pl_t)
+
+        col0 = []
+        at = 0
+        for width, code_loads, streamed in GROUPS:
+            col0.append(at)
+            at += width
+        assert at == COLS
+        units = []
+        for gi, (width, code_loads, streamed) in enumerate(GROUPS):
+            for ga, gb in code_loads:
+                units.append((gi, ga, gb))
+
+        code_tiles = {}
+
+        def load_codes(u):
+            gi, ga, gb = units[u]
+            width = GROUPS[gi][0]
+            lo = 2 * col0[gi]
+            hi = lo + 2 * width
+            size = 2 * width * (gb - ga)
+            if GROUPS[gi][2]:
+                wc = stream.tile([P, 2 * THIRD], U8, name="wc", tag="wc", align_bytes=64)
+            else:
+                wc = keep.tile([P, size], U8, name="wt%d" % u, tag="wt%d" % u, align_bytes=64)
+            if gb - ga == 1:
+                nc.sync.dma_start(out=wc[:, 0:size].bitcast(I32), in_=W_words[ga, :, lo:hi].bitcast(I32))
+            else:
+                nc.sync.dma_start(
+                    out=wc[:, 0:size].rearrange("p (g n) -> p g n", g=gb - ga).bitcast(I32),
+                    in_=W_words[ga:gb, :, lo:hi].rearrange("g p n -> p g n").bitcast(I32),
+                )
+            code_tiles[u] = wc
+
+        def load_scales(t):
+            for r in range(4):
+                nc.sync.dma_start(
+                    out=planes[t][r:P:32, :, :].bitcast(I32),
+                    in_=W_scales[:, r:16:4, t * THIRD : (t + 1) * THIRD].rearrange("g q n -> q g n").bitcast(I32),
+                )
+
+        def load_x():
+            nc.sync.dma_start(out=xw_raw[:].bitcast(I32), in_=x_words.rearrange("g p n -> p g n").bitcast(I32))
+            for r in range(4):
+                nc.sync.dma_start(
+                    out=xs_raw[r:P:32, :, :].bitcast(I32),
+                    in_=x_scales[:, r:16:4, :].rearrange("g q n -> q g n").bitcast(I32),
+                )
+
+        def permute_x():
+            for g in range(PASSES):
+                nc.vector.tensor_copy(
+                    out=xw[:, g, :].rearrange("p (l b t) -> p l b t", b=2, t=2),
+                    in_=xw_raw[:, g, :].rearrange("p (b l t) -> p l b t", b=2, t=2),
+                )
+            nc.vector.tensor_copy(
+                out=xs[:].rearrange("p g (l b) -> p g l b", b=2),
+                in_=xs_raw[:].rearrange("p g (b l) -> p g l b", b=2),
+            )
+
+        def load_unit(u):
+            for t in range(3):
+                if SCALES_BEFORE[t] == u:
+                    if t == 0:
+                        load_x()
+                        permute_x()
+                    else:
+                        nc.vector.memset(planes[t][:].bitcast(I32), 0)
+                    load_scales(t)
+            load_codes(u)
+
+        nc.vector.memset(xs_raw[:].bitcast(I32), 0)
+        nc.vector.memset(brows[:], 0.0)
+        nc.vector.memset(ss[:], 1.0)
+        nc.vector.memset(planes[0][:].bitcast(I32), 0)
+        make_identity(nc, ident[:])
+        nc.scalar.dma_start(out=brows[0 : COLS // BANK, :], in_=b.rearrange("(j n) -> j n", n=BANK))
+        nc.scalar.activation(out=warm[:], in_=ss[:, 0:1], func=AF.Sqrt)
+
+        for u in range(LOOKAHEAD):
+            load_unit(u)
+
+
+        def spread_bias(j):
+            pb = psum.tile([P, BANK], F32, name="pb", tag="pb", bufs=1)
+            nc.tensor.matmul(pb[:], lhsT=ident[:, j : j + 1].to_broadcast([P, P]), rhs=brows[:], start=True, stop=True)
+            nc.scalar.copy(out=bias[:, j * BANK : (j + 1) * BANK], in_=pb[:])
+
+        accs = {}
+
+        def multiply(u, g, k):
+            gi, ga, gb = units[u]
+            width = GROUPS[gi][0]
+            at_col, n = split_banks(width)[k]
+            if g == 0:
+                acc_new = psum.tile([P, BANK], F32, name="acc", tag="acc", bufs=7)
+                accs[(gi, k)] = acc_new
+            acc = accs[(gi, k)]
+            lo = col0[gi] + at_col
+            t = lo // THIRD
+            off = (g - ga) * 2 * width + 2 * at_col
+            nc.tensor.matmul_mx(
+                out=acc[:, 0:n],
+                lhsT=xw[:, g, :].bitcast(FP4X4),
+                lhsT_scale=xs[:, g, :],
+                rhs=code_tiles[u][:, off : off + 2 * n].bitcast(FP4X4),
+                rhs_scale=planes[t][:, g, lo - t * THIRD : lo - t * THIRD + n],
+                start=(g == 0),
+                stop=(g == PASSES - 1),
+            )
+
+        def y_cols(lo, hi):
+            t = lo // THIRD
+            assert (hi - 1) // THIRD == t
+            return ys[t][:].rearrange("p s c -> p (s c)")[:, lo - t * THIRD : hi - t * THIRD]
+
+        def seg_range(gi, k):
+            at_col, n = split_banks(GROUPS[gi][0])[k]
+            lo = col0[gi] + at_col
+            return lo // SEG, (lo + n) // SEG
+
+        def normed(s_lo, s_hi):
+            return [s for s in range(s_lo, s_hi) if s % 3 != 2]
+
+        def stage_a(gi, k):
+            at_col, n = split_banks(GROUPS[gi][0])[k]
+            lo = col0[gi] + at_col
+            nc.vector.tensor_tensor(out=y_cols(lo, lo + n), in0=accs[(gi, k)][:, 0:n], in1=bias[:, lo : lo + n], op=ALU.add)
+            s_lo, s_hi = seg_range(gi, k)
+            for s in normed(s_lo, s_hi):
+                nc.scalar.activation(
+                    out=junk[:], in_=y_cols(s * SEG, (s + 1) * SEG), func=AF.Square, accum_out=ss[:, s : s + 1]
+                )
+
+        def stage_b(gi, k):
+            s_lo, s_hi = seg_range(gi, k)
+            if len(normed(s_lo, s_hi)) == 0:
+                return
+            nc.vector.tensor_scalar(out=cl[:, s_lo:s_hi], in0=ss[:, s_lo:s_hi], scalar1=1e-24, scalar2=None, op0=ALU.max)
+            nc.vector.reciprocal(out=rc[:, s_lo:s_hi], in_=cl[:, s_lo:s_hi])
+            nc.scalar.activation(out=rn[:, s_lo:s_hi], in_=rc[:, s_lo:s_hi], func=AF.Sqrt)
+
+        stored = [0]
+
+        def store(s_lo, s_hi):
+            t = s_lo // (THIRD // SEG)
+            for kind in (2, 0, 1):
+                mine = [s for s in range(s_lo, s_hi) if s % 3 == kind]
+                if len(mine) == 0:
+                    continue
+                i0 = mine[0] - t * (THIRD // SEG)
+                h0 = mine[0] // 3
+                cnt = len(mine)
+                for bb in range(2):
+                    queue = nc.gpsimd if s_hi <= LAST_ON_POOL else nc.sync
+                    queue.dma_start(
+                        out=outs[kind][bb, h0 : h0 + cnt, :, :].rearrange("h l c -> l h c"),
+                        in_=ys[t][bb:P:2, i0 : i0 + 3 * (cnt - 1) + 1 : 3, :],
+                    )
+
+        def stage_c(gi, k):
+            s_lo, s_hi = seg_range(gi, k)
+            for s in normed(s_lo, s_hi):
+                seg = y_cols(s * SEG, (s + 1) * SEG)
+                nc.vector.tensor_scalar(out=seg, in0=seg, scalar1=rn[:, s : s + 1], scalar2=None, op0=ALU.mult)
+            for cut in STORE_CUTS:
+                if stored[0] < cut <= s_hi:
+                    store(stored[0], cut)
+                    stored[0] = cut
+
+        loaded = [LOOKAHEAD]
+        for u, (gi, ga, gb) in enumerate(units):
+            while loaded[0] < len(units) and (loaded[0] <= u + LOOKAHEAD or not GROUPS[units[loaded[0]][0]][2]):
+                load_unit(loaded[0])
+                loaded[0] += 1
+            if u < COLS // BANK:
+                spread_bias(u)
+            nb = len(split_banks(GROUPS[gi][0]))
+            for g in range(ga, gb):
+                if g < PASSES - 1:
+                    for k in range(nb):
+                        multiply(u, g, k)
+                else:
+                    for k in range(nb + 2):
+                        if k < nb:
+                            multiply(u, g, k)
+                            stage_a(gi, k)
+                        if 0 <= k - 1 < nb:
+                            stage_b(gi, k - 1)
+                        if 0 <= k - 2 < nb:
+                            stage_c(gi, k - 2)

@@ -29,7 +29,9 @@ GROUPS = (
     (512, ((0, 7),), False),
     (256, ((0, 4), (4, 7)), False),
 )
-SCALES_BEFORE = (3, 5, 12)
+SCALES_BEFORE = 2
+PLANE_PASSES = ((0, 3), (3, 6), (6, 7))
+SCALE_PIECES = ((0, 0, COLS), (1, 0, COLS), (2, 0, COLS // 2), (2, COLS // 2, COLS))
 STORE_CUTS = (8, 16, 24, 32, 40, 44, 46, 48)
 LAST_ON_POOL = 32
 CODE_BUFS = 8
@@ -75,7 +77,9 @@ def tile_selfattention_pa_kernel(tc, x_words, x_scales, W_words, W_scales, b, ou
         for t in range(3):
             y_t = keep.tile([P, THIRD // SEG, SEG], F32, name="y%d" % t, tag="y%d" % t)
             ys.append(y_t)
-            pl_t = keep.tile([P, PASSES, THIRD], U8, name="pl%d" % t, tag="pl%d" % t, align_bytes=64)
+            pl_t = keep.tile(
+                [P, PLANE_PASSES[t][1] - PLANE_PASSES[t][0], COLS], U8, name="pl%d" % t, tag="pl%d" % t, align_bytes=64
+            )
             planes.append(pl_t)
 
         col0 = []
@@ -110,11 +114,12 @@ def tile_selfattention_pa_kernel(tc, x_words, x_scales, W_words, W_scales, b, ou
                 )
             code_tiles[u] = wc
 
-        def load_scales(t):
+        def load_scales(t, lo, hi):
+            ga, gb = PLANE_PASSES[t]
             for r in range(4):
                 nc.sync.dma_start(
-                    out=planes[t][r:P:32, :, :].bitcast(I32),
-                    in_=W_scales[:, r:16:4, t * THIRD : (t + 1) * THIRD].rearrange("g q n -> q g n").bitcast(I32),
+                    out=planes[t][r:P:32, :, lo:hi].bitcast(I32),
+                    in_=W_scales[ga:gb, r:16:4, lo:hi].rearrange("g q n -> q g n").bitcast(I32),
                 )
 
         def load_x():
@@ -137,32 +142,32 @@ def tile_selfattention_pa_kernel(tc, x_words, x_scales, W_words, W_scales, b, ou
             )
 
         def load_unit(u):
-            for t in range(3):
-                if SCALES_BEFORE[t] == u:
-                    if t == 0:
-                        load_x()
-                        permute_x()
-                    else:
-                        nc.vector.memset(planes[t][:].bitcast(I32), 0)
-                    load_scales(t)
+            if u == SCALES_BEFORE:
+                for t, lo, hi in SCALE_PIECES:
+                    load_scales(t, lo, hi)
             load_codes(u)
+
+        def spread_bias(j):
+            pb = psum.tile([P, BANK], F32, name="pb", tag="acc", bufs=8)
+            nc.tensor.matmul(pb[:], lhsT=ident[:, j : j + 1].to_broadcast([P, P]), rhs=brows[:], start=True, stop=True)
+            nc.scalar.copy(out=bias[:, j * BANK : (j + 1) * BANK], in_=pb[:])
 
         nc.vector.memset(xs_raw[:].bitcast(I32), 0)
         nc.vector.memset(brows[:], 0.0)
         nc.vector.memset(ss[:], 1.0)
-        nc.vector.memset(planes[0][:].bitcast(I32), 0)
+        for t in range(3):
+            nc.vector.memset(planes[t][:].bitcast(I32), 0)
         make_identity(nc, ident[:])
         nc.scalar.dma_start(out=brows[0 : COLS // BANK, :], in_=b.rearrange("(j n) -> j n", n=BANK))
         nc.scalar.activation(out=warm[:], in_=ss[:, 0:1], func=AF.Sqrt)
 
+        load_x()
         for u in range(LOOKAHEAD):
             load_unit(u)
+        permute_x()
+        for j in range(COLS // BANK):
+            spread_bias(j)
 
-
-        def spread_bias(j):
-            pb = psum.tile([P, BANK], F32, name="pb", tag="pb", bufs=1)
-            nc.tensor.matmul(pb[:], lhsT=ident[:, j : j + 1].to_broadcast([P, P]), rhs=brows[:], start=True, stop=True)
-            nc.scalar.copy(out=bias[:, j * BANK : (j + 1) * BANK], in_=pb[:])
 
         accs = {}
 
@@ -171,18 +176,18 @@ def tile_selfattention_pa_kernel(tc, x_words, x_scales, W_words, W_scales, b, ou
             width = GROUPS[gi][0]
             at_col, n = split_banks(width)[k]
             if g == 0:
-                acc_new = psum.tile([P, BANK], F32, name="acc", tag="acc", bufs=7)
+                acc_new = psum.tile([P, BANK], F32, name="acc", tag="acc", bufs=8)
                 accs[(gi, k)] = acc_new
             acc = accs[(gi, k)]
             lo = col0[gi] + at_col
-            t = lo // THIRD
+            t = [i for i in range(3) if PLANE_PASSES[i][0] <= g < PLANE_PASSES[i][1]][0]
             off = (g - ga) * 2 * width + 2 * at_col
             nc.tensor.matmul_mx(
                 out=acc[:, 0:n],
                 lhsT=xw[:, g, :].bitcast(FP4X4),
                 lhsT_scale=xs[:, g, :],
                 rhs=code_tiles[u][:, off : off + 2 * n].bitcast(FP4X4),
-                rhs_scale=planes[t][:, g, lo - t * THIRD : lo - t * THIRD + n],
+                rhs_scale=planes[t][:, g - PLANE_PASSES[t][0], lo : lo + n],
                 start=(g == 0),
                 stop=(g == PASSES - 1),
             )
@@ -251,8 +256,6 @@ def tile_selfattention_pa_kernel(tc, x_words, x_scales, W_words, W_scales, b, ou
             while loaded[0] < len(units) and (loaded[0] <= u + LOOKAHEAD or not GROUPS[units[loaded[0]][0]][2]):
                 load_unit(loaded[0])
                 loaded[0] += 1
-            if u < COLS // BANK:
-                spread_bias(u)
             nb = len(split_banks(GROUPS[gi][0]))
             for g in range(ga, gb):
                 if g < PASSES - 1:

@@ -24,18 +24,23 @@ ONE_BY_ONE = tuple((g, g + 1) for g in range(PASSES))
 GROUPS = (
     (3584, ONE_BY_ONE, True),
     (3584, ONE_BY_ONE, True),
-    (1792, ONE_BY_ONE, True),
-    (1024, ONE_BY_ONE, False),
+    (1792, ((0, 2), (2, 4), (4, 6), (6, 7)), True),
+    (1024, ((0, 4), (4, 7)), False),
     (512, ((0, 7),), False),
-    (256, ((0, 4), (4, 7)), False),
+    (256, ((0, 7),), False),
 )
-SCALES_BEFORE = 2
-PLANE_PASSES = ((0, 3), (3, 6), (6, 7))
-SCALE_PIECES = ((0, 0, COLS), (1, 0, COLS), (2, 0, COLS // 2), (2, COLS // 2, COLS))
-STORE_CUTS = (8, 16, 24, 32, 40, 44, 46, 48)
+PLANE_COLS = ((0, THIRD), (THIRD, COLS))
+SCALES_BEFORE = 7
+SCALE_PIECES = (
+    (0, 0, 7, 0, THIRD),
+    (1, 0, 6, THIRD, COLS),
+    (1, 6, 7, THIRD, 2 * THIRD),
+    (1, 6, 7, 2 * THIRD, COLS),
+)
+STORE_CUTS = (16, 32, 40, 44, 48)
 LAST_ON_POOL = 32
 CODE_BUFS = 8
-LOOKAHEAD = 6
+LOOKAHEAD = 7
 
 
 def split_banks(width):
@@ -56,7 +61,7 @@ def tile_selfattention_pa_kernel(tc, x_words, x_scales, W_words, W_scales, b, ou
     with ExitStack() as ctx:
         keep = ctx.enter_context(tc.tile_pool(name="keep", bufs=1))
         stream = ctx.enter_context(tc.tile_pool(name="stream", bufs=CODE_BUFS))
-        psum = ctx.enter_context(tc.psum_pool(name="psum", bufs=1))
+        psum = ctx.enter_context(tc.psum_pool(name="psum", bufs=8))
         ctx.enter_context(tc.manual_schedule())
 
         xw_raw = keep.tile([P, PASSES, 256], U8, name="xw_raw", tag="xw_raw", align_bytes=64)
@@ -73,13 +78,12 @@ def tile_selfattention_pa_kernel(tc, x_words, x_scales, W_words, W_scales, b, ou
         junk = keep.tile([P, SEG], F32, name="junk", tag="junk")
         warm = keep.tile([P, 1], F32, name="warm", tag="warm")
         ys = []
-        planes = []
         for t in range(3):
             y_t = keep.tile([P, THIRD // SEG, SEG], F32, name="y%d" % t, tag="y%d" % t)
             ys.append(y_t)
-            pl_t = keep.tile(
-                [P, PLANE_PASSES[t][1] - PLANE_PASSES[t][0], COLS], U8, name="pl%d" % t, tag="pl%d" % t, align_bytes=64
-            )
+        planes = []
+        for t, (lo, hi) in enumerate(PLANE_COLS):
+            pl_t = keep.tile([P, PASSES, hi - lo], U8, name="pl%d" % t, tag="pl%d" % t, align_bytes=64)
             planes.append(pl_t)
 
         col0 = []
@@ -114,11 +118,11 @@ def tile_selfattention_pa_kernel(tc, x_words, x_scales, W_words, W_scales, b, ou
                 )
             code_tiles[u] = wc
 
-        def load_scales(t, lo, hi):
-            ga, gb = PLANE_PASSES[t]
+        def load_scales(t, ga, gb, lo, hi):
+            base = PLANE_COLS[t][0]
             for r in range(4):
                 nc.sync.dma_start(
-                    out=planes[t][r:P:32, :, lo:hi].bitcast(I32),
+                    out=planes[t][r:P:32, ga:gb, lo - base : hi - base].bitcast(I32),
                     in_=W_scales[ga:gb, r:16:4, lo:hi].rearrange("g q n -> q g n").bitcast(I32),
                 )
 
@@ -143,31 +147,29 @@ def tile_selfattention_pa_kernel(tc, x_words, x_scales, W_words, W_scales, b, ou
 
         def load_unit(u):
             if u == SCALES_BEFORE:
-                for t, lo, hi in SCALE_PIECES:
-                    load_scales(t, lo, hi)
+                for piece in SCALE_PIECES:
+                    load_scales(*piece)
             load_codes(u)
 
         def spread_bias(j):
-            pb = psum.tile([P, BANK], F32, name="pb", tag="acc", bufs=8)
+            pb = psum.tile([P, BANK], F32, name="pb", tag="acc")
             nc.tensor.matmul(pb[:], lhsT=ident[:, j : j + 1].to_broadcast([P, P]), rhs=brows[:], start=True, stop=True)
             nc.scalar.copy(out=bias[:, j * BANK : (j + 1) * BANK], in_=pb[:])
 
         nc.vector.memset(xs_raw[:].bitcast(I32), 0)
         nc.vector.memset(brows[:], 0.0)
         nc.vector.memset(ss[:], 1.0)
-        for t in range(3):
-            nc.vector.memset(planes[t][:].bitcast(I32), 0)
         make_identity(nc, ident[:])
         nc.scalar.dma_start(out=brows[0 : COLS // BANK, :], in_=b.rearrange("(j n) -> j n", n=BANK))
         nc.scalar.activation(out=warm[:], in_=ss[:, 0:1], func=AF.Sqrt)
-
         load_x()
-        for u in range(LOOKAHEAD):
-            load_unit(u)
         permute_x()
+        for pl_t in planes:
+            nc.vector.memset(pl_t[:].bitcast(I32), 0)
+        for u in range(LOOKAHEAD + 1):
+            load_unit(u)
         for j in range(COLS // BANK):
             spread_bias(j)
-
 
         accs = {}
 
@@ -176,18 +178,18 @@ def tile_selfattention_pa_kernel(tc, x_words, x_scales, W_words, W_scales, b, ou
             width = GROUPS[gi][0]
             at_col, n = split_banks(width)[k]
             if g == 0:
-                acc_new = psum.tile([P, BANK], F32, name="acc", tag="acc", bufs=8)
+                acc_new = psum.tile([P, BANK], F32, name="acc", tag="acc")
                 accs[(gi, k)] = acc_new
             acc = accs[(gi, k)]
             lo = col0[gi] + at_col
-            t = [i for i in range(3) if PLANE_PASSES[i][0] <= g < PLANE_PASSES[i][1]][0]
+            t = [i for i in range(len(PLANE_COLS)) if PLANE_COLS[i][0] <= lo < PLANE_COLS[i][1]][0]
             off = (g - ga) * 2 * width + 2 * at_col
             nc.tensor.matmul_mx(
                 out=acc[:, 0:n],
                 lhsT=xw[:, g, :].bitcast(FP4X4),
                 lhsT_scale=xs[:, g, :],
                 rhs=code_tiles[u][:, off : off + 2 * n].bitcast(FP4X4),
-                rhs_scale=planes[t][:, g - PLANE_PASSES[t][0], lo : lo + n],
+                rhs_scale=planes[t][:, g, lo - PLANE_COLS[t][0] : lo - PLANE_COLS[t][0] + n],
                 start=(g == 0),
                 stop=(g == PASSES - 1),
             )
@@ -251,7 +253,7 @@ def tile_selfattention_pa_kernel(tc, x_words, x_scales, W_words, W_scales, b, ou
                     store(stored[0], cut)
                     stored[0] = cut
 
-        loaded = [LOOKAHEAD]
+        loaded = [LOOKAHEAD + 1]
         for u, (gi, ga, gb) in enumerate(units):
             while loaded[0] < len(units) and (loaded[0] <= u + LOOKAHEAD or not GROUPS[units[loaded[0]][0]][2]):
                 load_unit(loaded[0])

@@ -38,7 +38,7 @@ SCALE_PIECES = (
     (1, 6, 7, 2 * THIRD, COLS),
 )
 STORE_CUTS = (16, 32, 40, 44, 48)
-LAST_ON_POOL = 32
+LAST_ON_ACT = 16
 CODE_BUFS = 8
 LOOKAHEAD = 7
 
@@ -237,7 +237,7 @@ def tile_selfattention_pa_kernel(tc, x_words, x_scales, W_words, W_scales, b, ou
                 h0 = mine[0] // 3
                 cnt = len(mine)
                 for bb in range(2):
-                    queue = nc.gpsimd if s_hi <= LAST_ON_POOL else nc.sync
+                    queue = nc.scalar if s_hi <= LAST_ON_ACT else nc.sync
                     queue.dma_start(
                         out=outs[kind][bb, h0 : h0 + cnt, :, :].rearrange("h l c -> l h c"),
                         in_=ys[t][bb:P:2, i0 : i0 + 3 * (cnt - 1) + 1 : 3, :],

@@ -25,9 +25,7 @@ GROUPS = (
     (3584, ONE_BY_ONE, True),
     (3584, ONE_BY_ONE, True),
     (1792, ((0, 2), (2, 4), (4, 6), (6, 7)), True),
-    (1024, ((0, 4), (4, 7)), False),
-    (512, ((0, 7),), False),
-    (256, ((0, 7),), False),
+    (1792, ((0, 2), (2, 4), (4, 6), (6, 7)), True),
 )
 PLANE_COLS = ((0, THIRD), (THIRD, COLS))
 SCALES_BEFORE = 7
@@ -37,8 +35,7 @@ SCALE_PIECES = (
     (1, 6, 7, THIRD, 2 * THIRD),
     (1, 6, 7, 2 * THIRD, COLS),
 )
-STORE_CUTS = (16, 32, 40, 44, 48)
-LAST_ON_ACT = 16
+STORE_CUTS = (32, 40, 48)
 CODE_BUFS = 8
 LOOKAHEAD = 7
 
@@ -77,10 +74,7 @@ def tile_selfattention_pa_kernel(tc, x_words, x_scales, W_words, W_scales, b, ou
         rn = keep.tile([P, SEGS], F32, name="rn", tag="rn")
         junk = keep.tile([P, SEG], F32, name="junk", tag="junk")
         warm = keep.tile([P, 1], F32, name="warm", tag="warm")
-        ys = []
-        for t in range(3):
-            y_t = keep.tile([P, THIRD // SEG, SEG], F32, name="y%d" % t, tag="y%d" % t)
-            ys.append(y_t)
+        y = keep.tile([P, SEGS, SEG], F32, name="y", tag="y")
         planes = []
         for t, (lo, hi) in enumerate(PLANE_COLS):
             pl_t = keep.tile([P, PASSES, hi - lo], U8, name="pl%d" % t, tag="pl%d" % t, align_bytes=64)
@@ -163,9 +157,9 @@ def tile_selfattention_pa_kernel(tc, x_words, x_scales, W_words, W_scales, b, ou
         nc.scalar.dma_start(out=brows[0 : COLS // BANK, :], in_=b.rearrange("(j n) -> j n", n=BANK))
         nc.scalar.activation(out=warm[:], in_=ss[:, 0:1], func=AF.Sqrt)
         load_x()
-        permute_x()
         for pl_t in planes:
             nc.vector.memset(pl_t[:].bitcast(I32), 0)
+        permute_x()
         for u in range(LOOKAHEAD + 1):
             load_unit(u)
         for j in range(COLS // BANK):
@@ -195,9 +189,7 @@ def tile_selfattention_pa_kernel(tc, x_words, x_scales, W_words, W_scales, b, ou
             )
 
         def y_cols(lo, hi):
-            t = lo // THIRD
-            assert (hi - 1) // THIRD == t
-            return ys[t][:].rearrange("p s c -> p (s c)")[:, lo - t * THIRD : hi - t * THIRD]
+            return y[:].rearrange("p s c -> p (s c)")[:, lo:hi]
 
         def seg_range(gi, k):
             at_col, n = split_banks(GROUPS[gi][0])[k]
@@ -226,38 +218,43 @@ def tile_selfattention_pa_kernel(tc, x_words, x_scales, W_words, W_scales, b, ou
             nc.scalar.activation(out=rn[:, s_lo:s_hi], in_=rc[:, s_lo:s_hi], func=AF.Sqrt)
 
         stored = [0]
+        done = [0]
+        loaded = [LOOKAHEAD + 1]
 
         def store(s_lo, s_hi):
-            t = s_lo // (THIRD // SEG)
             for kind in (2, 0, 1):
                 mine = [s for s in range(s_lo, s_hi) if s % 3 == kind]
                 if len(mine) == 0:
                     continue
-                i0 = mine[0] - t * (THIRD // SEG)
+                i0 = mine[0]
                 h0 = mine[0] // 3
                 cnt = len(mine)
                 for bb in range(2):
-                    queue = nc.scalar if s_hi <= LAST_ON_ACT else nc.sync
-                    queue.dma_start(
+                    nc.sync.dma_start(
                         out=outs[kind][bb, h0 : h0 + cnt, :, :].rearrange("h l c -> l h c"),
-                        in_=ys[t][bb:P:2, i0 : i0 + 3 * (cnt - 1) + 1 : 3, :],
+                        in_=y[bb:P:2, i0 : i0 + 3 * (cnt - 1) + 1 : 3, :],
                     )
 
         def stage_c(gi, k):
             s_lo, s_hi = seg_range(gi, k)
             for s in normed(s_lo, s_hi):
                 seg = y_cols(s * SEG, (s + 1) * SEG)
-                nc.vector.tensor_scalar(out=seg, in0=seg, scalar1=rn[:, s : s + 1], scalar2=None, op0=ALU.mult)
+                nc.scalar.activation(out=seg, in_=seg, func=AF.Copy, scale=rn[:, s : s + 1])
+            done[0] = s_hi
+
+        def store_what_is_done():
+            if loaded[0] < len(units):
+                return
             for cut in STORE_CUTS:
-                if stored[0] < cut <= s_hi:
+                if stored[0] < cut <= done[0]:
                     store(stored[0], cut)
                     stored[0] = cut
 
-        loaded = [LOOKAHEAD + 1]
         for u, (gi, ga, gb) in enumerate(units):
             while loaded[0] < len(units) and (loaded[0] <= u + LOOKAHEAD or not GROUPS[units[loaded[0]][0]][2]):
                 load_unit(loaded[0])
                 loaded[0] += 1
+            store_what_is_done()
             nb = len(split_banks(GROUPS[gi][0]))
             for g in range(ga, gb):
                 if g < PASSES - 1:
@@ -272,3 +269,4 @@ def tile_selfattention_pa_kernel(tc, x_words, x_scales, W_words, W_scales, b, ou
                             stage_b(gi, k - 1)
                         if 0 <= k - 2 < nb:
                             stage_c(gi, k - 2)
+                            store_what_is_done()

@@ -32,8 +32,7 @@ SCALES_BEFORE = 7
 SCALE_PIECES = (
     (0, 0, 7, 0, THIRD),
     (1, 0, 6, THIRD, COLS),
-    (1, 6, 7, THIRD, 2 * THIRD),
-    (1, 6, 7, 2 * THIRD, COLS),
+    (1, 6, 7, THIRD, COLS),
 )
 STORE_CUTS = (32, 40, 48)
 CODE_BUFS = 8
@@ -114,11 +113,12 @@ def tile_selfattention_pa_kernel(tc, x_words, x_scales, W_words, W_scales, b, ou
 
         def load_scales(t, ga, gb, lo, hi):
             base = PLANE_COLS[t][0]
-            for r in range(4):
-                nc.sync.dma_start(
-                    out=planes[t][r:P:32, ga:gb, lo - base : hi - base].bitcast(I32),
-                    in_=W_scales[ga:gb, r:16:4, lo:hi].rearrange("g q n -> q g n").bitcast(I32),
-                )
+            for half in range(2):
+                for r in range(4):
+                    nc.sync.dma_start(
+                        out=planes[t][32 * half + r : P : 64, ga:gb, lo - base : hi - base].bitcast(I32),
+                        in_=W_scales[ga:gb, 4 * half + r : 16 : 8, lo:hi].rearrange("g q n -> q g n").bitcast(I32),
+                    )
 
         def load_x():
             nc.sync.dma_start(out=xw_raw[:].bitcast(I32), in_=x_words.rearrange("g p n -> p g n").bitcast(I32))

@@ -34,7 +34,7 @@ SCALE_PIECES = (
     (1, 0, 6, THIRD, COLS),
     (1, 6, 7, THIRD, COLS),
 )
-STORE_CUTS = (32, 40, 48)
+STORE_CUTS = (32, 48)
 CODE_BUFS = 8
 LOOKAHEAD = 7
 

@@ -131,12 +131,12 @@ def tile_selfattention_pa_kernel(tc, x_words, x_scales, W_words, W_scales, b, ou
         def permute_x():
             for g in range(PASSES):
                 nc.vector.tensor_copy(
-                    out=xw[:, g, :].rearrange("p (l b t) -> p l b t", b=2, t=2),
-                    in_=xw_raw[:, g, :].rearrange("p (b l t) -> p l b t", b=2, t=2),
+                    out=xw[:, g, :].rearrange("p (m c t) -> p m c t", c=4, t=2),
+                    in_=xw_raw[:, g, :].rearrange("p (c m t) -> p m c t", c=4, t=2),
                 )
             nc.vector.tensor_copy(
-                out=xs[:].rearrange("p g (l b) -> p g l b", b=2),
-                in_=xs_raw[:].rearrange("p g (b l) -> p g l b", b=2),
+                out=xs[:].rearrange("p g (m c) -> p g m c", c=4),
+                in_=xs_raw[:].rearrange("p g (c m) -> p g m c", c=4),
             )
 
         def load_unit(u):
@@ -229,10 +229,11 @@ def tile_selfattention_pa_kernel(tc, x_words, x_scales, W_words, W_scales, b, ou
                 i0 = mine[0]
                 h0 = mine[0] // 3
                 cnt = len(mine)
-                for bb in range(2):
+                for c in range(4):
+                    l0 = 32 * (c % 2)
                     nc.sync.dma_start(
-                        out=outs[kind][bb, h0 : h0 + cnt, :, :].rearrange("h l c -> l h c"),
-                        in_=y[bb:P:2, i0 : i0 + 3 * (cnt - 1) + 1 : 3, :],
+                        out=outs[kind][c // 2, h0 : h0 + cnt, l0 : l0 + 32, :].rearrange("h l n -> l h n"),
+                        in_=y[c:P:4, i0 : i0 + 3 * (cnt - 1) + 1 : 3, :],
                     )
 
         def stage_c(gi, k):

from contextlib import ExitStack

import concourse.mybir as mybir
from concourse.masks import make_identity

F32 = mybir.dt.float32
BF16 = mybir.dt.bfloat16
U8 = mybir.dt.uint8
I32 = mybir.dt.int32
FP4X4 = mybir.dt.float4_e2m1fn_x4
AF = mybir.ActivationFunctionType
ALU = mybir.AluOpType

P = 128
PASSES = 7
COLS = 10752
SEG = 224
THIRD = 3584
SEGS = 48
BANK = 512
FLOPS = 2 * 128 * 3584 * 10752

ONE_BY_ONE = tuple((g, g + 1) for g in range(PASSES))
GROUPS = (
    (3584, ONE_BY_ONE, True),
    (3584, ONE_BY_ONE, True),
    (1792, ((0, 2), (2, 4), (4, 6), (6, 7)), True),
    (1792, ((0, 2), (2, 4), (4, 6), (6, 7)), True),
)
PLANE_COLS = ((0, THIRD), (THIRD, COLS))
SCALES_BEFORE = 7
SCALE_PIECES = (
    (0, 0, 7, 0, THIRD),
    (1, 0, 6, THIRD, COLS),
    (1, 6, 7, THIRD, COLS),
)
STORE_CUTS = (32, 48)
CODE_BUFS = 8
LOOKAHEAD = 7


def split_banks(width):
    banks = []
    at = 0
    for n in (512, 256, 128):
        while width - at >= n:
            banks.append((at, n))
            at += n
    assert at == width
    return banks


def tile_selfattention_pa_kernel(tc, x_words, x_scales, W_words, W_scales, b, out_0, out_1, out_2):
    nc = tc.nc
    outs = (out_0, out_1, out_2)

    with ExitStack() as ctx:
        keep = ctx.enter_context(tc.tile_pool(name="keep", bufs=1))
        stream = ctx.enter_context(tc.tile_pool(name="stream", bufs=CODE_BUFS))
        psum = ctx.enter_context(tc.psum_pool(name="psum", bufs=8))
        ctx.enter_context(tc.manual_schedule())

        xw_raw = keep.tile([P, PASSES, 256], U8, name="xw_raw", tag="xw_raw", align_bytes=64)
        xs_raw = keep.tile([P, PASSES, 128], U8, name="xs_raw", tag="xs_raw", align_bytes=64)
        xw = keep.tile([P, PASSES, 256], U8, name="xw", tag="xw", align_bytes=64)
        xs = keep.tile([P, PASSES, 128], U8, name="xs", tag="xs", align_bytes=64)
        ident = keep.tile([P, P], BF16, name="ident", tag="ident")
        brows = keep.tile([P, BANK], BF16, name="brows", tag="brows")
        bias = keep.tile([P, COLS], BF16, name="bias", tag="bias")
        ss = keep.tile([P, SEGS], F32, name="ss", tag="ss")
        cl = keep.tile([P, SEGS], F32, name="cl", tag="cl")
        rc = keep.tile([P, SEGS], F32, name="rc", tag="rc")
        rn = keep.tile([P, SEGS], F32, name="rn", tag="rn")
        junk = keep.tile([P, SEG], F32, name="junk", tag="junk")
        warm = keep.tile([P, 1], F32, name="warm", tag="warm")
        y = keep.tile([P, SEGS, SEG], F32, name="y", tag="y")
        planes = []
        for t, (lo, hi) in enumerate(PLANE_COLS):
            pl_t = keep.tile([P, PASSES, hi - lo], U8, name="pl%d" % t, tag="pl%d" % t, align_bytes=64)
            planes.append(pl_t)

        col0 = []
        at = 0
        for width, code_loads, streamed in GROUPS:
            col0.append(at)
            at += width
        assert at == COLS
        units = []
        for gi, (width, code_loads, streamed) in enumerate(GROUPS):
            for ga, gb in code_loads:
                units.append((gi, ga, gb))

        code_tiles = {}

        def load_codes(u):
            gi, ga, gb = units[u]
            width = GROUPS[gi][0]
            lo = 2 * col0[gi]
            hi = lo + 2 * width
            size = 2 * width * (gb - ga)
            if GROUPS[gi][2]:
                wc = stream.tile([P, 2 * THIRD], U8, name="wc", tag="wc", align_bytes=64)
            else:
                wc = keep.tile([P, size], U8, name="wt%d" % u, tag="wt%d" % u, align_bytes=64)
            if gb - ga == 1:
                nc.sync.dma_start(out=wc[:, 0:size].bitcast(I32), in_=W_words[ga, :, lo:hi].bitcast(I32))
            else:
                nc.sync.dma_start(
                    out=wc[:, 0:size].rearrange("p (g n) -> p g n", g=gb - ga).bitcast(I32),
                    in_=W_words[ga:gb, :, lo:hi].rearrange("g p n -> p g n").bitcast(I32),
                )
            code_tiles[u] = wc

        def load_scales(t, ga, gb, lo, hi):
            base = PLANE_COLS[t][0]
            for half in range(2):
                for r in range(4):
                    nc.sync.dma_start(
                        out=planes[t][32 * half + r : P : 64, ga:gb, lo - base : hi - base].bitcast(I32),
                        in_=W_scales[ga:gb, 4 * half + r : 16 : 8, lo:hi].rearrange("g q n -> q g n").bitcast(I32),
                    )

        def load_x():
            nc.sync.dma_start(out=xw_raw[:].bitcast(I32), in_=x_words.rearrange("g p n -> p g n").bitcast(I32))
            for r in range(4):
                nc.sync.dma_start(
                    out=xs_raw[r:P:32, :, :].bitcast(I32),
                    in_=x_scales[:, r:16:4, :].rearrange("g q n -> q g n").bitcast(I32),
                )

        def permute_x():
            for g in range(PASSES):
                nc.vector.tensor_copy(
                    out=xw[:, g, :].rearrange("p (m c t) -> p m c t", c=4, t=2),
                    in_=xw_raw[:, g, :].rearrange("p (c m t) -> p m c t", c=4, t=2),
                )
            nc.vector.tensor_copy(
                out=xs[:].rearrange("p g (m c) -> p g m c", c=4),
                in_=xs_raw[:].rearrange("p g (c m) -> p g m c", c=4),
            )

        def load_unit(u):
            if u == SCALES_BEFORE:
                for piece in SCALE_PIECES:
                    load_scales(*piece)
            load_codes(u)

        def spread_bias(j):
            pb = psum.tile([P, BANK], F32, name="pb", tag="acc")
            nc.tensor.matmul(pb[:], lhsT=ident[:, j : j + 1].to_broadcast([P, P]), rhs=brows[:], start=True, stop=True)
            nc.scalar.copy(out=bias[:, j * BANK : (j + 1) * BANK], in_=pb[:])

        nc.vector.memset(xs_raw[:].bitcast(I32), 0)
        nc.vector.memset(brows[:], 0.0)
        nc.vector.memset(ss[:], 1.0)
        make_identity(nc, ident[:])
        nc.scalar.dma_start(out=brows[0 : COLS // BANK, :], in_=b.rearrange("(j n) -> j n", n=BANK))
        nc.scalar.activation(out=warm[:], in_=ss[:, 0:1], func=AF.Sqrt)
        load_x()
        for pl_t in planes:
            nc.vector.memset(pl_t[:].bitcast(I32), 0)
        permute_x()
        for u in range(LOOKAHEAD + 1):
            load_unit(u)
        for j in range(COLS // BANK):
            spread_bias(j)

        accs = {}

        def multiply(u, g, k):
            gi, ga, gb = units[u]
            width = GROUPS[gi][0]
            at_col, n = split_banks(width)[k]
            if g == 0:
                acc_new = psum.tile([P, BANK], F32, name="acc", tag="acc")
                accs[(gi, k)] = acc_new
            acc = accs[(gi, k)]
            lo = col0[gi] + at_col
            t = [i for i in range(len(PLANE_COLS)) if PLANE_COLS[i][0] <= lo < PLANE_COLS[i][1]][0]
            off = (g - ga) * 2 * width + 2 * at_col
            nc.tensor.matmul_mx(
                out=acc[:, 0:n],
                lhsT=xw[:, g, :].bitcast(FP4X4),
                lhsT_scale=xs[:, g, :],
                rhs=code_tiles[u][:, off : off + 2 * n].bitcast(FP4X4),
                rhs_scale=planes[t][:, g, lo - PLANE_COLS[t][0] : lo - PLANE_COLS[t][0] + n],
                start=(g == 0),
                stop=(g == PASSES - 1),
            )

        def y_cols(lo, hi):
            return y[:].rearrange("p s c -> p (s c)")[:, lo:hi]

        def seg_range(gi, k):
            at_col, n = split_banks(GROUPS[gi][0])[k]
            lo = col0[gi] + at_col
            return lo // SEG, (lo + n) // SEG

        def normed(s_lo, s_hi):
            return [s for s in range(s_lo, s_hi) if s % 3 != 2]

        def stage_a(gi, k):
            at_col, n = split_banks(GROUPS[gi][0])[k]
            lo = col0[gi] + at_col
            nc.vector.tensor_tensor(out=y_cols(lo, lo + n), in0=accs[(gi, k)][:, 0:n], in1=bias[:, lo : lo + n], op=ALU.add)
            s_lo, s_hi = seg_range(gi, k)
            for s in normed(s_lo, s_hi):
                nc.scalar.activation(
                    out=junk[:], in_=y_cols(s * SEG, (s + 1) * SEG), func=AF.Square, accum_out=ss[:, s : s + 1]
                )

        def stage_b(gi, k):
            s_lo, s_hi = seg_range(gi, k)
            if len(normed(s_lo, s_hi)) == 0:
                return
            nc.vector.tensor_scalar(out=cl[:, s_lo:s_hi], in0=ss[:, s_lo:s_hi], scalar1=1e-24, scalar2=None, op0=ALU.max)
            nc.vector.reciprocal(out=rc[:, s_lo:s_hi], in_=cl[:, s_lo:s_hi])
            nc.scalar.activation(out=rn[:, s_lo:s_hi], in_=rc[:, s_lo:s_hi], func=AF.Sqrt)

        stored = [0]
        done = [0]
        loaded = [LOOKAHEAD + 1]

        def store(s_lo, s_hi):
            for kind in (2, 0, 1):
                mine = [s for s in range(s_lo, s_hi) if s % 3 == kind]
                if len(mine) == 0:
                    continue
                i0 = mine[0]
                h0 = mine[0] // 3
                cnt = len(mine)
                for c in range(4):
                    l0 = 32 * (c % 2)
                    nc.sync.dma_start(
                        out=outs[kind][c // 2, h0 : h0 + cnt, l0 : l0 + 32, :].rearrange("h l n -> l h n"),
                        in_=y[c:P:4, i0 : i0 + 3 * (cnt - 1) + 1 : 3, :],
                    )

        def stage_c(gi, k):
            s_lo, s_hi = seg_range(gi, k)
            for s in normed(s_lo, s_hi):
                seg = y_cols(s * SEG, (s + 1) * SEG)
                nc.scalar.activation(out=seg, in_=seg, func=AF.Copy, scale=rn[:, s : s + 1])
            done[0] = s_hi

        def store_what_is_done():
            if loaded[0] < len(units):
                return
            for cut in STORE_CUTS:
                if stored[0] < cut <= done[0]:
                    store(stored[0], cut)
                    stored[0] = cut

        for u, (gi, ga, gb) in enumerate(units):
            while loaded[0] < len(units) and (loaded[0] <= u + LOOKAHEAD or not GROUPS[units[loaded[0]][0]][2]):
                load_unit(loaded[0])
                loaded[0] += 1
            store_what_is_done()
            nb = len(split_banks(GROUPS[gi][0]))
            for g in range(ga, gb):
                if g < PASSES - 1:
                    for k in range(nb):
                        multiply(u, g, k)
                else:
                    for k in range(nb + 2):
                        if k < nb:
                            multiply(u, g, k)
                            stage_a(gi, k)
                        if 0 <= k - 1 < nb:
                            stage_b(gi, k - 1)
                        if 0 <= k - 2 < nb:
                            stage_c(gi, k - 2)
                            store_what_is_done()
